import numpy as np
import ml_dtypes


def mxq(x, axis, fmt="e4m3"):
    dtype, down = {"e4m3": (ml_dtypes.float8_e4m3fn, 7), "e5m2": (ml_dtypes.float8_e5m2, 14)}[fmt]
    v = np.moveaxis(np.asarray(x, np.float32).astype(ml_dtypes.bfloat16).astype(np.float64), axis, -1)
    blocks = v.reshape(v.shape[:-1] + (-1, 32))
    amax = np.abs(blocks).max(-1, keepdims=True)
    byte = np.maximum(np.where(amax > 0, np.frexp(amax)[1] - 1 + 127, 0) - down, 1)
    scale = np.exp2(byte - 127.0)
    codes = (blocks / scale).astype(np.float32).astype(dtype).astype(np.float64)
    return np.moveaxis((codes * scale).reshape(v.shape), -1, axis)


WIDE = False


def mx_kscale(k):
    if not WIDE:
        return np.ones(k)
    levels = np.array([10, -10, 5, -5, 0])
    a = np.random.permutation(np.resize(levels, k // 512 * 4)).reshape(k // 512, 4)
    idx = np.arange(k)
    return np.exp2(a[idx // 512, idx % 128 // 32])


BF16 = ml_dtypes.bfloat16


def bf(x):
    return np.asarray(x, np.float32).astype(BF16)


def f64(x):
    return np.asarray(x).astype(np.float64)


E2M1 = np.array([0.0, 0.5, 1.0, 1.5, 2.0, 3.0, 4.0, 6.0, -0.0, -0.5, -1.0, -1.5, -2.0, -3.0, -4.0, -6.0])


def pack_weight(w, fmt):
    k, n = w.shape
    w = f64(bf(w)).reshape(k // 32, 32, n)
    amax = np.abs(w).max(1)
    if fmt == "e4m3":
        byte = np.frexp(amax)[1] - 1 + 127 - 7
    else:
        mant, ex = np.frexp(amax / 6.0)
        byte = np.where(mant > 0.5, ex, ex - 1) + 127
    byte = np.clip(np.where(amax > 0, byte, 1), 1, 254)
    scaled = (w * np.exp2(127.0 - byte)[:, None, :]).reshape(k, n).astype(np.float32)
    by_word = np.ascontiguousarray(scaled.reshape(k // 512, 128, 4, n).transpose(0, 1, 3, 2))
    if fmt == "e4m3":
        words = by_word.astype(ml_dtypes.float8_e4m3fn).view(np.uint8)
    else:
        c = by_word.astype(ml_dtypes.float4_e2m1fn).view(np.uint8) & 0xF
        words = c[..., 0::2] | (c[..., 1::2] << 4)
    return np.ascontiguousarray(words), np.ascontiguousarray(byte.astype(np.uint8).reshape(k // 512, 16, n))


def unpack_weight(words, scales, fmt):
    g, p, n, _ = words.shape
    if fmt == "e4m3":
        vals = np.ascontiguousarray(words).view(ml_dtypes.float8_e4m3fn).astype(np.float64)
    else:
        nib = np.empty((g, p, n, 4), np.uint8)
        nib[..., 0::2] = words & 0xF
        nib[..., 1::2] = words >> 4
        vals = E2M1[nib]
    vals = vals * np.repeat(np.exp2(scales.astype(np.float64) - 127.0), 8, axis=1)[..., None]
    return vals.transpose(0, 1, 3, 2).reshape(g * 512, n)


B, C, H, W, K, O = 1, 512, 32, 32, 3, 512
P = C * K * K
PAD = 1
G = 32
FMT = "e4m3"


def im2col(a):
    a_pad = np.pad(a, ((0, 0), (0, 0), (PAD, PAD), (PAD, PAD)), mode="reflect")
    cols = np.stack([a_pad[:, :, kh:kh + H, kw:kw + W] for kh in range(K) for kw in range(K)], axis=2)
    cols = cols.reshape(B, P, H * W)
    return np.swapaxes(cols, 1, 2)


def setup_inputs():
    u = np.unique(mx_kscale(P))
    t = u[np.arange(C // G) % len(u)]
    sc = np.repeat(t, G).reshape(1, C, 1, 1)
    sp = np.repeat(t, G * K * K).reshape(P, 1)
    lam = 1.0 if len(u) == 1 else 0.0
    g = 2.0 ** np.round(0.5 * np.log2(np.mean(t ** 2)))
    amp = 0.5 + 1.5 * np.random.random_sample((B, 1, H, W))
    off = 0.6 + 0.4 * np.random.standard_normal((B, 1, H, W))
    bound = np.sqrt(6.0 / P)
    z = np.random.standard_normal((B, C, H, W))
    z[:, 1::2] = lam * z[:, 1::2] - (1.0 - lam) * z[:, 0::2]
    a = bf((z * amp + off * lam) * sc)
    words, scales = pack_weight(np.random.uniform(-bound, bound, (P, O)) * g / sp, FMT)
    return {"a": a,
            "conv_kernel_words": words,
            "conv_kernel_scales": scales}


def reference(a, conv_kernel_words, conv_kernel_scales):
    patches = im2col(f64(a))
    mean = np.mean(patches, axis=-1, keepdims=True)
    std = np.std(patches, axis=-1, keepdims=True, ddof=1)
    normed = (patches - mean) / std
    out = mxq(normed, 2, "e4m3") @ unpack_weight(conv_kernel_words, conv_kernel_scales, FMT)
    return np.swapaxes(out, 1, 2).reshape(B, O, H, W)

@@ -1,0 +1,304 @@
+import concourse.mybir as mybir
+from concourse.masks import make_identity
+
+BF16 = mybir.dt.bfloat16
+F32 = mybir.dt.float32
+I32 = mybir.dt.int32
+U32 = mybir.dt.uint32
+U8 = mybir.dt.uint8
+FP8X4 = mybir.dt.float8_e4m3fn_x4
+ALU = mybir.AluOpType
+ACT = mybir.ActivationFunctionType
+AXIS = mybir.AxisListType
+
+P = 128
+C = 512
+SIDE = 32
+PIXELS = SIDE * SIDE
+TAPS = 9
+O = 512
+PATCH = C * TAPS
+PACK = 4
+PASSES = PATCH // (P * PACK)
+PAIR = 2
+HALVES = PACK // PAIR
+
+PIXEL_TILES = PIXELS // P
+TILE_ROWS = P // SIDE
+PADDED_ROWS = SIDE + 2
+IMAGE = PADDED_ROWS * SIDE
+
+BANK_BF16 = 1024
+BANK_F32 = 512
+BANK_CHANNELS = (BANK_BF16 - P) // (TAPS - 1)
+CHANNEL_TILES = -(-C // BANK_CHANNELS)
+
+GROUP_TILES = 2
+GROUP_PIXELS = GROUP_TILES * P
+GROUPS = PIXELS // GROUP_PIXELS
+O_TILES = O // P
+
+FLOPS = 2 * PIXELS * PATCH * O
+
+
+def channel_tile(b):
+    first = b * BANK_CHANNELS
+    count = min(BANK_CHANNELS, C - first)
+    loaded_from = min(first, C - P)
+    return first, count, loaded_from
+
+
+def tile_norm_conv_kernel(tc, a, conv_kernel_words, conv_kernel_scales, out):
+    nc = tc.nc
+    a_rows = a.rearrange("b c h w -> (b c) (h w)")
+    out_rows = out.rearrange("b o h w -> (b o) (h w)")
+
+    with (
+        tc.tile_pool(name="keep", bufs=1) as keep,
+        tc.tile_pool(name="work", bufs=2) as work,
+        tc.psum_pool(name="first_banks", bufs=4) as first_banks,
+        tc.psum_pool(name="second_banks", bufs=2) as second_banks,
+        tc.psum_pool(name="sum_banks", bufs=2) as sum_banks,
+    ):
+        shifted = keep.tile([P, 3, CHANNEL_TILES, IMAGE], BF16)
+        for b in range(CHANNEL_TILES):
+            c0 = channel_tile(b)[2]
+            nc.sync.dma_start(out=shifted[:, 1, b, SIDE : SIDE + PIXELS], in_=a_rows[c0 : c0 + P, :])
+        for b in range(CHANNEL_TILES):
+            c0 = channel_tile(b)[2]
+            nc.sync.dma_start(out=shifted[:, 0, b, SIDE + 1 : SIDE + PIXELS], in_=a_rows[c0 : c0 + P, 0 : PIXELS - 1])
+        for b in range(CHANNEL_TILES):
+            c0 = channel_tile(b)[2]
+            nc.sync.dma_start(out=shifted[:, 2, b, SIDE : SIDE + PIXELS - 1], in_=a_rows[c0 : c0 + P, 1:PIXELS])
+
+        w_scales = keep.tile([P, PASSES, O], U8, align_bytes=64)
+        nc.vector.memset(w_scales[:].rearrange("p g o -> p (g o)").bitcast(I32), 0)
+        for quadrant in range(4):
+            nc.sync.dma_start(
+                out=w_scales[32 * quadrant : 32 * quadrant + 4, :, :].bitcast(I32),
+                in_=conv_kernel_scales[:, 4 * quadrant : 4 * quadrant + 4, :]
+                .rearrange("g q o -> q g o")
+                .bitcast(I32),
+            )
+        w_words = keep.tile([P, PASSES, O], U32, align_bytes=64)
+        nc.sync.dma_start(
+            out=w_words[:].bitcast(I32),
+            in_=conv_kernel_words.rearrange("g r o t -> r g (o t)").bitcast(I32),
+        )
+
+        ident_bf = keep.tile([P, P], BF16)
+        make_identity(nc, ident_bf[:])
+        ident_f32 = keep.tile([P, P], F32)
+        make_identity(nc, ident_f32[:])
+        turn = channel_tile(CHANNEL_TILES - 1)[0] - channel_tile(CHANNEL_TILES - 1)[2]
+        ident_turned = keep.tile([P, P], BF16)
+        nc.vector.tensor_copy(out=ident_turned[:, 0 : P - turn], in_=ident_bf[:, turn:P])
+        nc.vector.tensor_copy(out=ident_turned[:, P - turn : P], in_=ident_bf[:, 0:turn])
+
+        ident_rows = ident_f32[:].rearrange("p (y x) -> p y x", x=SIDE)
+        ident_padded = keep.tile([P, TILE_ROWS, SIDE + 2], F32)
+        nc.vector.tensor_copy(out=ident_padded[:, :, 1 : SIDE + 1], in_=ident_rows)
+        nc.vector.tensor_copy(out=ident_padded[:, :, 0:1], in_=ident_rows[:, :, 1:2])
+        nc.vector.tensor_copy(out=ident_padded[:, :, SIDE + 1 : SIDE + 2], in_=ident_rows[:, :, SIDE - 2 : SIDE - 1])
+        band = keep.tile([P, 3 * TILE_ROWS + 2, SIDE], F32)
+        nc.vector.memset(band[:], 0.0)
+        across = band[:, TILE_ROWS + 1 : 2 * TILE_ROWS + 1, :]
+        nc.vector.tensor_add(out=across, in0=ident_padded[:, :, 0:SIDE], in1=ident_padded[:, :, 1 : SIDE + 1])
+        nc.vector.tensor_add(out=across, in0=across, in1=ident_padded[:, :, 2 : SIDE + 2])
+        box = keep.tile([P, 3 * TILE_ROWS, SIDE], F32)
+        nc.vector.tensor_add(out=box[:], in0=band[:, 0 : 3 * TILE_ROWS, :], in1=band[:, 1 : 3 * TILE_ROWS + 1, :])
+        nc.vector.tensor_add(out=box[:], in0=box[:], in1=band[:, 2 : 3 * TILE_ROWS + 2, :])
+        box_to_tile_above = box[:, 0:TILE_ROWS, :].rearrange("p y x -> p (y x)")
+        box_same_tile = box[:, TILE_ROWS : 2 * TILE_ROWS, :].rearrange("p y x -> p (y x)")
+        box_to_tile_below = box[:, 2 * TILE_ROWS : 3 * TILE_ROWS, :].rearrange("p y x -> p (y x)")
+        reflect_top = keep.tile([P, TILE_ROWS, SIDE], F32)
+        nc.vector.memset(reflect_top[:], 0.0)
+        nc.vector.tensor_copy(out=reflect_top[:, 0:1, :], in_=across[:, 1:2, :])
+        reflect_bottom = keep.tile([P, TILE_ROWS, SIDE], F32)
+        nc.vector.memset(reflect_bottom[:], 0.0)
+        nc.vector.tensor_copy(
+            out=reflect_bottom[:, TILE_ROWS - 1 : TILE_ROWS, :], in_=across[:, TILE_ROWS - 2 : TILE_ROWS - 1, :]
+        )
+
+        grid = shifted[:].rearrange("p k b (y x) -> p k b y x", x=SIDE)
+        nc.vector.tensor_copy(out=grid[:, 0, :, 1 : SIDE + 1, 0:1], in_=grid[:, 1, :, 1 : SIDE + 1, 1:2])
+        nc.vector.tensor_copy(
+            out=grid[:, 2, :, 1 : SIDE + 1, SIDE - 1 : SIDE], in_=grid[:, 1, :, 1 : SIDE + 1, SIDE - 2 : SIDE - 1]
+        )
+        nc.vector.tensor_copy(out=grid[:, :, :, 0, :], in_=grid[:, :, :, 2, :])
+        nc.vector.tensor_copy(out=grid[:, :, :, SIDE + 1, :], in_=grid[:, :, :, SIDE - 1, :])
+
+        pixel_sums = keep.tile([P, 2, 16], F32)
+        nc.vector.memset(pixel_sums[:], 0.0)
+        for T in range(PIXEL_TILES):
+            start = (TILE_ROWS * T + 1) * SIDE
+            by_pixel = first_banks.tile([P, BANK_BF16], BF16, tag="first")
+            for b in range(CHANNEL_TILES):
+                c0 = channel_tile(b)[2]
+                nc.tensor.transpose(
+                    out=by_pixel[:, c0 : c0 + P], in_=shifted[:, 1, b, start : start + P], identity=ident_bf[:]
+                )
+            pixel_values = work.tile([P, C], BF16)
+            nc.vector.tensor_copy(out=pixel_values[:], in_=by_pixel[:, 0:C])
+            nc.vector.reduce_sum(out=pixel_sums[:, 0, 1 + T : 2 + T], in_=pixel_values[:], axis=AXIS.X)
+            squares = work.tile([P, C], BF16)
+            nc.scalar.activation(
+                out=squares[:], in_=pixel_values[:], func=ACT.Square, accum_out=pixel_sums[:, 1, 1 + T : 2 + T]
+            )
+
+        patch_sums_bank = sum_banks.tile([P, BANK_F32], F32, tag="sums")
+        patch_sums_psum = patch_sums_bank[:, 0 : 2 * PIXEL_TILES].rearrange("p (s T) -> p s T", s=2)
+        nc.tensor.matmul(
+            out=patch_sums_psum, lhsT=box_same_tile, rhs=pixel_sums[:, :, 1 : 1 + PIXEL_TILES], start=True, stop=False
+        )
+        nc.tensor.matmul(
+            out=patch_sums_psum, lhsT=box_to_tile_below, rhs=pixel_sums[:, :, 0:PIXEL_TILES], start=False, stop=False
+        )
+        nc.tensor.matmul(
+            out=patch_sums_psum, lhsT=box_to_tile_above, rhs=pixel_sums[:, :, 2 : 2 + PIXEL_TILES], start=False, stop=False
+        )
+        nc.tensor.matmul(
+            out=patch_sums_psum[:, :, 0:1],
+            lhsT=reflect_top[:].rearrange("p y x -> p (y x)"),
+            rhs=pixel_sums[:, :, 1:2],
+            start=False,
+            stop=False,
+        )
+        nc.tensor.matmul(
+            out=patch_sums_psum[:, :, PIXEL_TILES - 1 : PIXEL_TILES],
+            lhsT=reflect_bottom[:].rearrange("p y x -> p (y x)"),
+            rhs=pixel_sums[:, :, PIXEL_TILES : PIXEL_TILES + 1],
+            start=False,
+            stop=True,
+        )
+        patch_sums = keep.tile([P, 2, PIXEL_TILES], F32)
+        nc.vector.tensor_copy(out=patch_sums[:], in_=patch_sums_psum)
+        mean = keep.tile([P, PIXEL_TILES], F32)
+        nc.vector.tensor_scalar_mul(out=mean[:], in0=patch_sums[:, 0, :], scalar1=1.0 / PATCH)
+        deviations = keep.tile([P, PIXEL_TILES], F32)
+        nc.vector.tensor_mul(out=deviations[:], in0=patch_sums[:, 0, :], in1=mean[:])
+        nc.vector.tensor_sub(out=deviations[:], in0=patch_sums[:, 1, :], in1=deviations[:])
+        std = keep.tile([P, PIXEL_TILES], F32)
+        nc.scalar.activation(out=std[:], in_=deviations[:], func=ACT.Sqrt, scale=1.0 / (PATCH - 1))
+        inv_std = keep.tile([P, PIXEL_TILES], F32)
+        nc.vector.reciprocal(out=inv_std[:], in_=std[:])
+        shift = keep.tile([P, PIXEL_TILES], F32)
+        nc.vector.scalar_tensor_tensor(
+            out=shift[:], in0=mean[:], scalar=-1.0, in1=inv_std[:], op0=ALU.mult, op1=ALU.mult
+        )
+
+        codes = keep.tile([P, GROUPS, PASSES, GROUP_PIXELS], U32, align_bytes=64)
+        code_scales = keep.tile([P, GROUPS, PASSES, GROUP_PIXELS], U8, align_bytes=64)
+        normed_tiles = {}
+        grouped_tiles = {}
+
+        def window(T, tap, b):
+            kh, kw = divmod(tap, 3)
+            start = (TILE_ROWS * T + kh) * SIDE
+            return shifted[:, kw, b, start : start + P]
+
+        def patches_to_pixels(T):
+            normed = work.tile([P, PATCH], BF16, tag="normed")
+            normed_tiles[T] = normed
+            by_channel = normed[:].rearrange("p (c k) -> p c k", k=TAPS)
+            for b in range(CHANNEL_TILES):
+                first, count, loaded_from = channel_tile(b)
+                own_channels_first = ident_bf if first == loaded_from else ident_turned
+                bank = first_banks.tile([P, BANK_BF16], BF16, tag="first")
+                for tap in range(TAPS):
+                    nc.tensor.transpose(
+                        out=bank[:, tap * BANK_CHANNELS : tap * BANK_CHANNELS + P],
+                        in_=window(T, tap, b),
+                        identity=own_channels_first[:],
+                    )
+                raw = bank[:, 0 : TAPS * BANK_CHANNELS].rearrange("p (k c) -> p c k", k=TAPS)[:, 0:count, :]
+                if count == BANK_CHANNELS:
+                    nc.scalar.activation(
+                        out=by_channel[:, first : first + count, :],
+                        in_=raw,
+                        func=ACT.Identity,
+                        bias=shift[:, T : T + 1],
+                        scale=inv_std[:, T : T + 1],
+                    )
+                else:
+                    nc.vector.tensor_scalar(
+                        out=by_channel[:, first : first + count, :],
+                        in0=raw,
+                        scalar1=inv_std[:, T : T + 1],
+                        scalar2=shift[:, T : T + 1],
+                        op0=ALU.mult,
+                        op1=ALU.add,
+                    )
+
+        def words_to_partitions(T):
+            group, half = divmod(T, GROUP_TILES)
+            if half == 0:
+                grouped_tiles[group] = work.tile(
+                    [P, PASSES, GROUP_PIXELS * PACK], BF16, tag="grouped", align_bytes=64, name="grouped"
+                )
+            grouped_pairs = grouped_tiles[group][:].bitcast(F32).rearrange("p g (n u) -> p g n u", u=HALVES)
+            normed_pairs = normed_tiles[T][:].bitcast(F32)
+            pass_pairs = P * HALVES
+            passes_in_bank = BANK_F32 // pass_pairs
+            for g0 in range(0, PASSES, passes_in_bank):
+                n = min(passes_in_bank, PASSES - g0)
+                bank = second_banks.tile([P, BANK_F32], F32, tag="second")
+                for i in range(n):
+                    for u in range(HALVES):
+                        nc.tensor.transpose(
+                            out=bank[:, (i * HALVES + u) * P : (i * HALVES + u + 1) * P],
+                            in_=normed_pairs[:, (g0 + i) * pass_pairs + u : (g0 + i + 1) * pass_pairs : HALVES],
+                            identity=ident_f32[:],
+                        )
+                nc.vector.tensor_copy(
+                    out=grouped_pairs[:, g0 : g0 + n, half * P : (half + 1) * P, :],
+                    in_=bank[:, 0 : n * pass_pairs].rearrange("p (g u n) -> p g n u", g=n, u=HALVES),
+                )
+
+        def quantise(group):
+            grouped = grouped_tiles[group]
+            passes_in_call = 4
+            for g0 in range(0, PASSES, passes_in_call):
+                n = min(passes_in_call, PASSES - g0)
+                nc.vector.quantize_mx(
+                    out=codes[:, group, g0 : g0 + n, :].rearrange("p g n -> p (g n)").bitcast(FP8X4),
+                    scales=code_scales[:, group, g0 : g0 + n, :].rearrange("p g n -> p (g n)"),
+                    in_=grouped[:, g0 : g0 + n, :].rearrange("p g n -> p (g n)"),
+                )
+
+        def multiply(group):
+            columns = slice(group * GROUP_PIXELS, (group + 1) * GROUP_PIXELS)
+            in_bank = BANK_F32 // GROUP_PIXELS
+            for o0 in range(0, O_TILES, in_bank):
+                bank = sum_banks.tile([P, BANK_F32], F32, tag="sums")
+                sums = bank[:].rearrange("p (i n) -> p i n", i=in_bank)
+                for i in range(in_bank):
+                    o_columns = slice((o0 + i) * P, (o0 + i + 1) * P)
+                    for g in range(PASSES):
+                        nc.tensor.matmul_mx(
+                            out=sums[:, i, :],
+                            lhsT=w_words[:, g, o_columns].bitcast(FP8X4),
+                            lhsT_scale=w_scales[:, g, o_columns],
+                            rhs=codes[:, group, g, :].bitcast(FP8X4),
+                            rhs_scale=code_scales[:, group, g, :],
+                            start=(g == 0),
+                            stop=(g == PASSES - 1),
+                        )
+                result = work.tile([P, in_bank, GROUP_PIXELS], F32)
+                nc.scalar.copy(out=result[:], in_=sums)
+                nc.sync.dma_start(
+                    out=out_rows[o0 * P : (o0 + in_bank) * P, columns].rearrange("(i o) n -> o i n", o=P),
+                    in_=result[:],
+                )
+
+        patches_to_pixels(0)
+        for T in range(PIXEL_TILES):
+            if T + 1 < PIXEL_TILES:
+                patches_to_pixels(T + 1)
+            words_to_partitions(T)
+            group, half = divmod(T, GROUP_TILES)
+            if half == GROUP_TILES - 1:
+                quantise(group)
+                if group > 0:
+                    multiply(group - 1)
+        multiply(GROUPS - 1)

@@ -33,10 +33,9 @@ BANK_F32 = 512
 BANK_CHANNELS = (BANK_BF16 - P) // (TAPS - 1)
 CHANNEL_TILES = -(-C // BANK_CHANNELS)
 
-GROUP_TILES = 2
-GROUP_PIXELS = GROUP_TILES * P
-GROUPS = PIXELS // GROUP_PIXELS
 O_TILES = O // P
+BANK_PASSES = BANK_F32 // (P * HALVES)
+SECOND_BANKS = -(-PASSES // BANK_PASSES)
 
 FLOPS = 2 * PIXELS * PATCH * O
 
@@ -121,12 +120,12 @@ def tile_norm_conv_kernel(tc, a, conv_kernel_words, conv_kernel_scales, out):
         )
 
         grid = shifted[:].rearrange("p k b (y x) -> p k b y x", x=SIDE)
-        nc.vector.tensor_copy(out=grid[:, 0, :, 1 : SIDE + 1, 0:1], in_=grid[:, 1, :, 1 : SIDE + 1, 1:2])
-        nc.vector.tensor_copy(
+        nc.gpsimd.tensor_copy(out=grid[:, 0, :, 1 : SIDE + 1, 0:1], in_=grid[:, 1, :, 1 : SIDE + 1, 1:2])
+        nc.gpsimd.tensor_copy(
             out=grid[:, 2, :, 1 : SIDE + 1, SIDE - 1 : SIDE], in_=grid[:, 1, :, 1 : SIDE + 1, SIDE - 2 : SIDE - 1]
         )
-        nc.vector.tensor_copy(out=grid[:, :, :, 0, :], in_=grid[:, :, :, 2, :])
-        nc.vector.tensor_copy(out=grid[:, :, :, SIDE + 1, :], in_=grid[:, :, :, SIDE - 1, :])
+        nc.gpsimd.tensor_copy(out=grid[:, :, :, 0, :], in_=grid[:, :, :, 2, :])
+        nc.gpsimd.tensor_copy(out=grid[:, :, :, SIDE + 1, :], in_=grid[:, :, :, SIDE - 1, :])
 
         pixel_sums = keep.tile([P, 2, 16], F32)
         nc.vector.memset(pixel_sums[:], 0.0)
@@ -187,118 +186,108 @@ def tile_norm_conv_kernel(tc, a, conv_kernel_words, conv_kernel_scales, out):
             out=shift[:], in0=mean[:], scalar=-1.0, in1=inv_std[:], op0=ALU.mult, op1=ALU.mult
         )
 
-        codes = keep.tile([P, GROUPS, PASSES, GROUP_PIXELS], U32, align_bytes=64)
-        code_scales = keep.tile([P, GROUPS, PASSES, GROUP_PIXELS], U8, align_bytes=64)
+        codes = keep.tile([P, PIXEL_TILES, PASSES, P], U32, align_bytes=64)
+        code_scales = keep.tile([P, PIXEL_TILES, PASSES, P], U8, align_bytes=64)
         normed_tiles = {}
         grouped_tiles = {}
+        sum_tiles = {}
 
-        def window(T, tap, b):
-            kh, kw = divmod(tap, 3)
-            start = (TILE_ROWS * T + kh) * SIDE
-            return shifted[:, kw, b, start : start + P]
-
-        def patches_to_pixels(T):
-            normed = work.tile([P, PATCH], BF16, tag="normed")
-            normed_tiles[T] = normed
-            by_channel = normed[:].rearrange("p (c k) -> p c k", k=TAPS)
-            for b in range(CHANNEL_TILES):
-                first, count, loaded_from = channel_tile(b)
-                own_channels_first = ident_bf if first == loaded_from else ident_turned
-                bank = first_banks.tile([P, BANK_BF16], BF16, tag="first")
-                for tap in range(TAPS):
-                    nc.tensor.transpose(
-                        out=bank[:, tap * BANK_CHANNELS : tap * BANK_CHANNELS + P],
-                        in_=window(T, tap, b),
-                        identity=own_channels_first[:],
-                    )
-                raw = bank[:, 0 : TAPS * BANK_CHANNELS].rearrange("p (k c) -> p c k", k=TAPS)[:, 0:count, :]
-                if count == BANK_CHANNELS:
-                    nc.scalar.activation(
-                        out=by_channel[:, first : first + count, :],
-                        in_=raw,
-                        func=ACT.Identity,
-                        bias=shift[:, T : T + 1],
-                        scale=inv_std[:, T : T + 1],
-                    )
-                else:
-                    nc.vector.tensor_scalar(
-                        out=by_channel[:, first : first + count, :],
-                        in0=raw,
-                        scalar1=inv_std[:, T : T + 1],
-                        scalar2=shift[:, T : T + 1],
-                        op0=ALU.mult,
-                        op1=ALU.add,
-                    )
-
-        def words_to_partitions(T):
-            group, half = divmod(T, GROUP_TILES)
-            if half == 0:
-                grouped_tiles[group] = work.tile(
-                    [P, PASSES, GROUP_PIXELS * PACK], BF16, tag="grouped", align_bytes=64, name="grouped"
+        def patches_to_pixels(T, b):
+            if b == 0:
+                normed_tiles[T] = work.tile([P, PATCH], BF16, tag="normed", name="normed")
+            by_channel = normed_tiles[T][:].rearrange("p (c k) -> p c k", k=TAPS)
+            first, count, loaded_from = channel_tile(b)
+            own_channels_first = ident_bf if first == loaded_from else ident_turned
+            bank = first_banks.tile([P, BANK_BF16], BF16, tag="first")
+            for tap in range(TAPS):
+                kh, kw = divmod(tap, 3)
+                start = (TILE_ROWS * T + kh) * SIDE
+                nc.tensor.transpose(
+                    out=bank[:, tap * BANK_CHANNELS : tap * BANK_CHANNELS + P],
+                    in_=shifted[:, kw, b, start : start + P],
+                    identity=own_channels_first[:],
                 )
-            grouped_pairs = grouped_tiles[group][:].bitcast(F32).rearrange("p g (n u) -> p g n u", u=HALVES)
+            raw = bank[:, 0 : TAPS * BANK_CHANNELS].rearrange("p (k c) -> p c k", k=TAPS)[:, 0:count, :]
+            if count == BANK_CHANNELS:
+                nc.scalar.activation(
+                    out=by_channel[:, first : first + count, :],
+                    in_=raw,
+                    func=ACT.Identity,
+                    bias=shift[:, T : T + 1],
+                    scale=inv_std[:, T : T + 1],
+                )
+            else:
+                nc.vector.tensor_scalar(
+                    out=by_channel[:, first : first + count, :],
+                    in0=raw,
+                    scalar1=inv_std[:, T : T + 1],
+                    scalar2=shift[:, T : T + 1],
+                    op0=ALU.mult,
+                    op1=ALU.add,
+                )
+
+        def words_to_partitions(T, j):
+            if j == 0:
+                grouped_tiles[T] = work.tile([P, PASSES, P * PACK], BF16, tag="grouped", align_bytes=64, name="grouped")
+            grouped_pairs = grouped_tiles[T][:].bitcast(F32).rearrange("p g (n u) -> p g n u", u=HALVES)
             normed_pairs = normed_tiles[T][:].bitcast(F32)
             pass_pairs = P * HALVES
-            passes_in_bank = BANK_F32 // pass_pairs
-            for g0 in range(0, PASSES, passes_in_bank):
-                n = min(passes_in_bank, PASSES - g0)
-                bank = second_banks.tile([P, BANK_F32], F32, tag="second")
-                for i in range(n):
-                    for u in range(HALVES):
-                        nc.tensor.transpose(
-                            out=bank[:, (i * HALVES + u) * P : (i * HALVES + u + 1) * P],
-                            in_=normed_pairs[:, (g0 + i) * pass_pairs + u : (g0 + i + 1) * pass_pairs : HALVES],
-                            identity=ident_f32[:],
-                        )
-                nc.vector.tensor_copy(
-                    out=grouped_pairs[:, g0 : g0 + n, half * P : (half + 1) * P, :],
-                    in_=bank[:, 0 : n * pass_pairs].rearrange("p (g u n) -> p g n u", g=n, u=HALVES),
-                )
+            g0 = j * BANK_PASSES
+            n = min(BANK_PASSES, PASSES - g0)
+            bank = second_banks.tile([P, BANK_F32], F32, tag="second")
+            for i in range(n):
+                for u in range(HALVES):
+                    nc.tensor.transpose(
+                        out=bank[:, (i * HALVES + u) * P : (i * HALVES + u + 1) * P],
+                        in_=normed_pairs[:, (g0 + i) * pass_pairs + u : (g0 + i + 1) * pass_pairs : HALVES],
+                        identity=ident_f32[:],
+                    )
+            nc.vector.tensor_copy(
+                out=grouped_pairs[:, g0 : g0 + n, :, :],
+                in_=bank[:, 0 : n * pass_pairs].rearrange("p (g u n) -> p g n u", g=n, u=HALVES),
+            )
 
-        def quantise(group):
-            grouped = grouped_tiles[group]
-            passes_in_call = 4
+        def quantise(T):
+            passes_in_call = 8
             for g0 in range(0, PASSES, passes_in_call):
                 n = min(passes_in_call, PASSES - g0)
                 nc.vector.quantize_mx(
-                    out=codes[:, group, g0 : g0 + n, :].rearrange("p g n -> p (g n)").bitcast(FP8X4),
-                    scales=code_scales[:, group, g0 : g0 + n, :].rearrange("p g n -> p (g n)"),
-                    in_=grouped[:, g0 : g0 + n, :].rearrange("p g n -> p (g n)"),
+                    out=codes[:, T, g0 : g0 + n, :].rearrange("p g n -> p (g n)").bitcast(FP8X4),
+                    scales=code_scales[:, T, g0 : g0 + n, :].rearrange("p g n -> p (g n)"),
+                    in_=grouped_tiles[T][:, g0 : g0 + n, :].rearrange("p g n -> p (g n)"),
                 )
 
-        def multiply(group):
-            columns = slice(group * GROUP_PIXELS, (group + 1) * GROUP_PIXELS)
-            in_bank = BANK_F32 // GROUP_PIXELS
-            for o0 in range(0, O_TILES, in_bank):
-                bank = sum_banks.tile([P, BANK_F32], F32, tag="sums")
-                sums = bank[:].rearrange("p (i n) -> p i n", i=in_bank)
-                for i in range(in_bank):
-                    o_columns = slice((o0 + i) * P, (o0 + i + 1) * P)
-                    for g in range(PASSES):
-                        nc.tensor.matmul_mx(
-                            out=sums[:, i, :],
-                            lhsT=w_words[:, g, o_columns].bitcast(FP8X4),
-                            lhsT_scale=w_scales[:, g, o_columns],
-                            rhs=codes[:, group, g, :].bitcast(FP8X4),
-                            rhs_scale=code_scales[:, group, g, :],
-                            start=(g == 0),
-                            stop=(g == PASSES - 1),
-                        )
-                result = work.tile([P, in_bank, GROUP_PIXELS], F32)
-                nc.scalar.copy(out=result[:], in_=sums)
+        def multiply(T, i):
+            if i == 0:
+                sum_tiles[T] = sum_banks.tile([P, O_TILES, P], F32, tag="sums", name="sums")
+            sums = sum_tiles[T]
+            o_columns = slice(i * P, (i + 1) * P)
+            for g in range(PASSES):
+                nc.tensor.matmul_mx(
+                    out=sums[:, i, :],
+                    lhsT=w_words[:, g, o_columns].bitcast(FP8X4),
+                    lhsT_scale=w_scales[:, g, o_columns],
+                    rhs=codes[:, T, g, :].bitcast(FP8X4),
+                    rhs_scale=code_scales[:, T, g, :],
+                    start=(g == 0),
+                    stop=(g == PASSES - 1),
+                )
+            if i == O_TILES - 1:
+                result = work.tile([P, O_TILES, P], F32)
+                nc.scalar.copy(out=result[:], in_=sums[:])
                 nc.sync.dma_start(
-                    out=out_rows[o0 * P : (o0 + in_bank) * P, columns].rearrange("(i o) n -> o i n", o=P),
-                    in_=result[:],
+                    out=out_rows[:, T * P : (T + 1) * P].rearrange("(i o) n -> o i n", o=P), in_=result[:]
                 )
 
-        patches_to_pixels(0)
-        for T in range(PIXEL_TILES):
-            if T + 1 < PIXEL_TILES:
-                patches_to_pixels(T + 1)
-            words_to_partitions(T)
-            group, half = divmod(T, GROUP_TILES)
-            if half == GROUP_TILES - 1:
-                quantise(group)
-                if group > 0:
-                    multiply(group - 1)
-        multiply(GROUPS - 1)
+        assert CHANNEL_TILES == SECOND_BANKS == O_TILES + 1
+        with tc.manual_schedule():
+            for T in range(-1, PIXEL_TILES + 1):
+                for step in range(CHANNEL_TILES):
+                    if T + 1 < PIXEL_TILES:
+                        patches_to_pixels(T + 1, step)
+                    if 0 <= T < PIXEL_TILES:
+                        words_to_partitions(T, step)
+                    if T >= 1 and step >= 1:
+                        multiply(T - 1, step - 1)
+                if 0 <= T < PIXEL_TILES:
+                    quantise(T)

@@ -55,9 +55,9 @@ def tile_norm_conv_kernel(tc, a, conv_kernel_words, conv_kernel_scales, out):
     with (
         tc.tile_pool(name="keep", bufs=1) as keep,
         tc.tile_pool(name="work", bufs=2) as work,
-        tc.psum_pool(name="first_banks", bufs=4) as first_banks,
+        tc.psum_pool(name="first_banks", bufs=CHANNEL_TILES) as first_banks,
         tc.psum_pool(name="second_banks", bufs=2) as second_banks,
-        tc.psum_pool(name="sum_banks", bufs=2) as sum_banks,
+        tc.psum_pool(name="sum_banks", bufs=1) as sum_banks,
     ):
         shifted = keep.tile([P, 3, CHANNEL_TILES, IMAGE], BF16)
         for b in range(CHANNEL_TILES):
@@ -192,39 +192,42 @@ def tile_norm_conv_kernel(tc, a, conv_kernel_words, conv_kernel_scales, out):
         grouped_tiles = {}
         sum_tiles = {}
 
-        def patches_to_pixels(T, b):
-            if b == 0:
-                normed_tiles[T] = work.tile([P, PATCH], BF16, tag="normed", name="normed")
-            by_channel = normed_tiles[T][:].rearrange("p (c k) -> p c k", k=TAPS)
-            first, count, loaded_from = channel_tile(b)
-            own_channels_first = ident_bf if first == loaded_from else ident_turned
-            bank = first_banks.tile([P, BANK_BF16], BF16, tag="first")
+        def patches_to_pixels(T):
+            normed = work.tile([P, PATCH], BF16, tag="normed")
+            normed_tiles[T] = normed
+            by_channel = normed[:].rearrange("p (c k) -> p c k", k=TAPS)
+            banks = [first_banks.tile([P, BANK_BF16], BF16, tag="first", name="bank") for b in range(CHANNEL_TILES)]
             for tap in range(TAPS):
                 kh, kw = divmod(tap, 3)
                 start = (TILE_ROWS * T + kh) * SIDE
-                nc.tensor.transpose(
-                    out=bank[:, tap * BANK_CHANNELS : tap * BANK_CHANNELS + P],
-                    in_=shifted[:, kw, b, start : start + P],
-                    identity=own_channels_first[:],
-                )
-            raw = bank[:, 0 : TAPS * BANK_CHANNELS].rearrange("p (k c) -> p c k", k=TAPS)[:, 0:count, :]
-            if count == BANK_CHANNELS:
-                nc.scalar.activation(
-                    out=by_channel[:, first : first + count, :],
-                    in_=raw,
-                    func=ACT.Identity,
-                    bias=shift[:, T : T + 1],
-                    scale=inv_std[:, T : T + 1],
-                )
-            else:
-                nc.vector.tensor_scalar(
-                    out=by_channel[:, first : first + count, :],
-                    in0=raw,
-                    scalar1=inv_std[:, T : T + 1],
-                    scalar2=shift[:, T : T + 1],
-                    op0=ALU.mult,
-                    op1=ALU.add,
-                )
+                for b in range(CHANNEL_TILES):
+                    first, count, loaded_from = channel_tile(b)
+                    own_channels_first = ident_bf if first == loaded_from else ident_turned
+                    nc.tensor.transpose(
+                        out=banks[b][:, tap * BANK_CHANNELS : tap * BANK_CHANNELS + P],
+                        in_=shifted[:, kw, b, start : start + P],
+                        identity=own_channels_first[:],
+                    )
+            for b in range(CHANNEL_TILES):
+                first, count, loaded_from = channel_tile(b)
+                raw = banks[b][:, 0 : TAPS * BANK_CHANNELS].rearrange("p (k c) -> p c k", k=TAPS)[:, 0:count, :]
+                if count == BANK_CHANNELS:
+                    nc.scalar.activation(
+                        out=by_channel[:, first : first + count, :],
+                        in_=raw,
+                        func=ACT.Identity,
+                        bias=shift[:, T : T + 1],
+                        scale=inv_std[:, T : T + 1],
+                    )
+                else:
+                    nc.vector.tensor_scalar(
+                        out=by_channel[:, first : first + count, :],
+                        in0=raw,
+                        scalar1=inv_std[:, T : T + 1],
+                        scalar2=shift[:, T : T + 1],
+                        op0=ALU.mult,
+                        op1=ALU.add,
+                    )
 
         def words_to_partitions(T, j):
             if j == 0:
@@ -279,12 +282,12 @@ def tile_norm_conv_kernel(tc, a, conv_kernel_words, conv_kernel_scales, out):
                     out=out_rows[:, T * P : (T + 1) * P].rearrange("(i o) n -> o i n", o=P), in_=result[:]
                 )
 
-        assert CHANNEL_TILES == SECOND_BANKS == O_TILES + 1
+        assert SECOND_BANKS == O_TILES + 1
         with tc.manual_schedule():
             for T in range(-1, PIXEL_TILES + 1):
-                for step in range(CHANNEL_TILES):
-                    if T + 1 < PIXEL_TILES:
-                        patches_to_pixels(T + 1, step)
+                if T + 1 < PIXEL_TILES:
+                    patches_to_pixels(T + 1)
+                for step in range(SECOND_BANKS):
                     if 0 <= T < PIXEL_TILES:
                         words_to_partitions(T, step)
                     if T >= 1 and step >= 1:

@@ -36,6 +36,13 @@ CHANNEL_TILES = -(-C // BANK_CHANNELS)
 O_TILES = O // P
 BANK_PASSES = BANK_F32 // (P * HALVES)
 SECOND_BANKS = -(-PASSES // BANK_PASSES)
+SECOND_POOL = 2
+
+SCALAR_CHANNEL_TILES = 4
+
+HALF_TILES = PIXEL_TILES // 2
+STATS = 6
+PARITY_COUNT = C // 2
 
 FLOPS = 2 * PIXELS * PATCH * O
 
@@ -56,19 +63,32 @@ def tile_norm_conv_kernel(tc, a, conv_kernel_words, conv_kernel_scales, out):
         tc.tile_pool(name="keep", bufs=1) as keep,
         tc.tile_pool(name="work", bufs=2) as work,
         tc.psum_pool(name="first_banks", bufs=CHANNEL_TILES) as first_banks,
-        tc.psum_pool(name="second_banks", bufs=2) as second_banks,
+        tc.psum_pool(name="second_banks", bufs=SECOND_POOL) as second_banks,
         tc.psum_pool(name="sum_banks", bufs=1) as sum_banks,
+        tc.manual_schedule(),
     ):
         shifted = keep.tile([P, 3, CHANNEL_TILES, IMAGE], BF16)
-        for b in range(CHANNEL_TILES):
-            c0 = channel_tile(b)[2]
-            nc.sync.dma_start(out=shifted[:, 1, b, SIDE : SIDE + PIXELS], in_=a_rows[c0 : c0 + P, :])
-        for b in range(CHANNEL_TILES):
-            c0 = channel_tile(b)[2]
-            nc.sync.dma_start(out=shifted[:, 0, b, SIDE + 1 : SIDE + PIXELS], in_=a_rows[c0 : c0 + P, 0 : PIXELS - 1])
-        for b in range(CHANNEL_TILES):
-            c0 = channel_tile(b)[2]
-            nc.sync.dma_start(out=shifted[:, 2, b, SIDE : SIDE + PIXELS - 1], in_=a_rows[c0 : c0 + P, 1:PIXELS])
+        grid = shifted[:].rearrange("p k b (y x) -> p k b y x", x=SIDE)
+
+        def load_rows(first_row, end_row):
+            for kw in (1, 0, 2):
+                move = kw - 1
+                lo = first_row * SIDE + max(move, 0)
+                hi = end_row * SIDE + min(move, 0)
+                for b in range(CHANNEL_TILES):
+                    c0 = channel_tile(b)[2]
+                    nc.sync.dma_start(
+                        out=shifted[:, kw, b, SIDE + lo - move : SIDE + hi - move], in_=a_rows[c0 : c0 + P, lo:hi]
+                    )
+
+        def mend_columns(first_row, end_row):
+            rows = slice(first_row + 1, end_row + 1)
+            nc.gpsimd.tensor_copy(out=grid[:, 0, :, rows, 0:1], in_=grid[:, 1, :, rows, 1:2])
+            nc.gpsimd.tensor_copy(out=grid[:, 2, :, rows, SIDE - 1 : SIDE], in_=grid[:, 1, :, rows, SIDE - 2 : SIDE - 1])
+
+        split_row = (HALF_TILES + 1) * TILE_ROWS
+        load_rows(0, split_row)
+        load_rows(split_row, SIDE)
 
         w_scales = keep.tile([P, PASSES, O], U8, align_bytes=64)
         nc.vector.memset(w_scales[:].rearrange("p g o -> p (g o)").bitcast(I32), 0)
@@ -84,6 +104,10 @@ def tile_norm_conv_kernel(tc, a, conv_kernel_words, conv_kernel_scales, out):
             out=w_words[:].bitcast(I32),
             in_=conv_kernel_words.rearrange("g r o t -> r g (o t)").bitcast(I32),
         )
+
+        one = keep.tile([P, 1], F32)
+        nc.vector.memset(one[:], 1.0)
+        nc.scalar.activation(out=one[:], in_=one[:], func=ACT.Sqrt)
 
         ident_bf = keep.tile([P, P], BF16)
         make_identity(nc, ident_bf[:])
@@ -119,72 +143,90 @@ def tile_norm_conv_kernel(tc, a, conv_kernel_words, conv_kernel_scales, out):
             out=reflect_bottom[:, TILE_ROWS - 1 : TILE_ROWS, :], in_=across[:, TILE_ROWS - 2 : TILE_ROWS - 1, :]
         )
 
-        grid = shifted[:].rearrange("p k b (y x) -> p k b y x", x=SIDE)
-        nc.gpsimd.tensor_copy(out=grid[:, 0, :, 1 : SIDE + 1, 0:1], in_=grid[:, 1, :, 1 : SIDE + 1, 1:2])
-        nc.gpsimd.tensor_copy(
-            out=grid[:, 2, :, 1 : SIDE + 1, SIDE - 1 : SIDE], in_=grid[:, 1, :, 1 : SIDE + 1, SIDE - 2 : SIDE - 1]
-        )
-        nc.gpsimd.tensor_copy(out=grid[:, :, :, 0, :], in_=grid[:, :, :, 2, :])
-        nc.gpsimd.tensor_copy(out=grid[:, :, :, SIDE + 1, :], in_=grid[:, :, :, SIDE - 1, :])
+        pixel_stats = keep.tile([P, PIXEL_TILES + 2, STATS], F32)
+        nc.vector.memset(pixel_stats[:], 0.0)
+        by_parity = pixel_stats[:].rearrange("p T (e s) -> p T e s", e=2)
+        inv_std = keep.tile([P, PIXEL_TILES], F32)
+        shift = keep.tile([P, PIXEL_TILES], F32)
 
-        pixel_sums = keep.tile([P, 2, 16], F32)
-        nc.vector.memset(pixel_sums[:], 0.0)
-        for T in range(PIXEL_TILES):
-            start = (TILE_ROWS * T + 1) * SIDE
-            by_pixel = first_banks.tile([P, BANK_BF16], BF16, tag="first")
-            for b in range(CHANNEL_TILES):
-                c0 = channel_tile(b)[2]
-                nc.tensor.transpose(
-                    out=by_pixel[:, c0 : c0 + P], in_=shifted[:, 1, b, start : start + P], identity=ident_bf[:]
-                )
-            pixel_values = work.tile([P, C], BF16)
-            nc.vector.tensor_copy(out=pixel_values[:], in_=by_pixel[:, 0:C])
-            nc.vector.reduce_sum(out=pixel_sums[:, 0, 1 + T : 2 + T], in_=pixel_values[:], axis=AXIS.X)
-            squares = work.tile([P, C], BF16)
-            nc.scalar.activation(
-                out=squares[:], in_=pixel_values[:], func=ACT.Square, accum_out=pixel_sums[:, 1, 1 + T : 2 + T]
+        def pixel_statistics(first_tile, end_tile):
+            for T in range(first_tile, end_tile):
+                start = (TILE_ROWS * T + 1) * SIDE
+                by_pixel = second_banks.tile([P, BANK_BF16], BF16, tag="second")
+                for b in range(CHANNEL_TILES):
+                    c0 = channel_tile(b)[2]
+                    nc.tensor.transpose(
+                        out=by_pixel[:, c0 : c0 + P], in_=shifted[:, 1, b, start : start + P], identity=ident_bf[:]
+                    )
+                nc.vector.bn_stats(out=pixel_stats[:, 1 + T, :], in_=by_pixel[:, 0:C])
+            tiles = slice(1 + first_tile, 1 + end_tile)
+            squared_means = work.tile([P, end_tile - first_tile, 2], F32, tag="squared_means")
+            nc.vector.tensor_mul(out=squared_means[:], in0=by_parity[:, tiles, :, 1], in1=by_parity[:, tiles, :, 1])
+            nc.vector.scalar_tensor_tensor(
+                out=by_parity[:, tiles, :, 2],
+                in0=squared_means[:],
+                scalar=float(PARITY_COUNT),
+                in1=by_parity[:, tiles, :, 2],
+                op0=ALU.mult,
+                op1=ALU.add,
             )
 
-        patch_sums_bank = sum_banks.tile([P, BANK_F32], F32, tag="sums")
-        patch_sums_psum = patch_sums_bank[:, 0 : 2 * PIXEL_TILES].rearrange("p (s T) -> p s T", s=2)
-        nc.tensor.matmul(
-            out=patch_sums_psum, lhsT=box_same_tile, rhs=pixel_sums[:, :, 1 : 1 + PIXEL_TILES], start=True, stop=False
-        )
-        nc.tensor.matmul(
-            out=patch_sums_psum, lhsT=box_to_tile_below, rhs=pixel_sums[:, :, 0:PIXEL_TILES], start=False, stop=False
-        )
-        nc.tensor.matmul(
-            out=patch_sums_psum, lhsT=box_to_tile_above, rhs=pixel_sums[:, :, 2 : 2 + PIXEL_TILES], start=False, stop=False
-        )
-        nc.tensor.matmul(
-            out=patch_sums_psum[:, :, 0:1],
-            lhsT=reflect_top[:].rearrange("p y x -> p (y x)"),
-            rhs=pixel_sums[:, :, 1:2],
-            start=False,
-            stop=False,
-        )
-        nc.tensor.matmul(
-            out=patch_sums_psum[:, :, PIXEL_TILES - 1 : PIXEL_TILES],
-            lhsT=reflect_bottom[:].rearrange("p y x -> p (y x)"),
-            rhs=pixel_sums[:, :, PIXEL_TILES : PIXEL_TILES + 1],
-            start=False,
-            stop=True,
-        )
-        patch_sums = keep.tile([P, 2, PIXEL_TILES], F32)
-        nc.vector.tensor_copy(out=patch_sums[:], in_=patch_sums_psum)
-        mean = keep.tile([P, PIXEL_TILES], F32)
-        nc.vector.tensor_scalar_mul(out=mean[:], in0=patch_sums[:, 0, :], scalar1=1.0 / PATCH)
-        deviations = keep.tile([P, PIXEL_TILES], F32)
-        nc.vector.tensor_mul(out=deviations[:], in0=patch_sums[:, 0, :], in1=mean[:])
-        nc.vector.tensor_sub(out=deviations[:], in0=patch_sums[:, 1, :], in1=deviations[:])
-        std = keep.tile([P, PIXEL_TILES], F32)
-        nc.scalar.activation(out=std[:], in_=deviations[:], func=ACT.Sqrt, scale=1.0 / (PATCH - 1))
-        inv_std = keep.tile([P, PIXEL_TILES], F32)
-        nc.vector.reciprocal(out=inv_std[:], in_=std[:])
-        shift = keep.tile([P, PIXEL_TILES], F32)
-        nc.vector.scalar_tensor_tensor(
-            out=shift[:], in0=mean[:], scalar=-1.0, in1=inv_std[:], op0=ALU.mult, op1=ALU.mult
-        )
+        def patch_statistics(first_tile, end_tile):
+            n = end_tile - first_tile
+            bank = sum_banks.tile([P, BANK_F32], F32, tag="sums")
+            boxed = bank[:, 0 : 4 * n].rearrange("p (T e s) -> p T e s", e=2, s=2)
+
+            def neighbours(offset):
+                return by_parity[:, 1 + first_tile + offset : 1 + end_tile + offset, :, 1:3]
+
+            terms = [
+                (boxed, box_same_tile, neighbours(0)),
+                (boxed, box_to_tile_below, neighbours(-1)),
+                (boxed, box_to_tile_above, neighbours(1)),
+            ]
+            if first_tile == 0:
+                terms.append((boxed[:, 0:1], reflect_top[:].rearrange("p y x -> p (y x)"), neighbours(0)[:, 0:1]))
+            if end_tile == PIXEL_TILES:
+                terms.append(
+                    (boxed[:, n - 1 : n], reflect_bottom[:].rearrange("p y x -> p (y x)"), neighbours(0)[:, n - 1 : n])
+                )
+            for i, (target, matrix, numbers) in enumerate(terms):
+                nc.tensor.matmul(out=target, lhsT=matrix, rhs=numbers, start=(i == 0), stop=(i == len(terms) - 1))
+            patch = work.tile([P, n, 2], F32, tag="patch")
+            nc.vector.tensor_reduce(out=patch[:], in_=boxed.rearrange("p T e s -> p T s e"), axis=AXIS.X, op=ALU.add)
+            deviations = work.tile([P, n], F32, tag="deviations")
+            nc.vector.tensor_mul(out=deviations[:], in0=patch[:, :, 0], in1=patch[:, :, 0])
+            nc.vector.scalar_tensor_tensor(
+                out=deviations[:],
+                in0=deviations[:],
+                scalar=-float(PARITY_COUNT * PARITY_COUNT) / PATCH,
+                in1=patch[:, :, 1],
+                op0=ALU.mult,
+                op1=ALU.add,
+            )
+            std = work.tile([P, n], F32, tag="std")
+            nc.scalar.activation(out=std[:], in_=deviations[:], func=ACT.Sqrt, scale=1.0 / (PATCH - 1))
+            nc.vector.reciprocal(out=inv_std[:, first_tile:end_tile], in_=std[:])
+            nc.vector.scalar_tensor_tensor(
+                out=shift[:, first_tile:end_tile],
+                in0=patch[:, :, 0],
+                scalar=-float(PARITY_COUNT) / PATCH,
+                in1=inv_std[:, first_tile:end_tile],
+                op0=ALU.mult,
+                op1=ALU.mult,
+            )
+
+        def prepare_upper_half():
+            mend_columns(0, split_row)
+            pixel_statistics(0, HALF_TILES + 1)
+            nc.vector.tensor_copy(out=grid[:, :, :, 0, :], in_=grid[:, :, :, 2, :])
+            patch_statistics(0, HALF_TILES)
+
+        def prepare_lower_half():
+            mend_columns(split_row, SIDE)
+            pixel_statistics(HALF_TILES + 1, PIXEL_TILES)
+            nc.vector.tensor_copy(out=grid[:, :, :, SIDE + 1, :], in_=grid[:, :, :, SIDE - 1, :])
+            patch_statistics(HALF_TILES, PIXEL_TILES)
 
         codes = keep.tile([P, PIXEL_TILES, PASSES, P], U32, align_bytes=64)
         code_scales = keep.tile([P, PIXEL_TILES, PASSES, P], U8, align_bytes=64)
@@ -211,7 +253,7 @@ def tile_norm_conv_kernel(tc, a, conv_kernel_words, conv_kernel_scales, out):
             for b in range(CHANNEL_TILES):
                 first, count, loaded_from = channel_tile(b)
                 raw = banks[b][:, 0 : TAPS * BANK_CHANNELS].rearrange("p (k c) -> p c k", k=TAPS)[:, 0:count, :]
-                if count == BANK_CHANNELS:
+                if b < SCALAR_CHANNEL_TILES:
                     nc.scalar.activation(
                         out=by_channel[:, first : first + count, :],
                         in_=raw,
@@ -282,15 +324,18 @@ def tile_norm_conv_kernel(tc, a, conv_kernel_words, conv_kernel_scales, out):
                     out=out_rows[:, T * P : (T + 1) * P].rearrange("(i o) n -> o i n", o=P), in_=result[:]
                 )
 
-        assert SECOND_BANKS == O_TILES + 1
-        with tc.manual_schedule():
-            for T in range(-1, PIXEL_TILES + 1):
-                if T + 1 < PIXEL_TILES:
-                    patches_to_pixels(T + 1)
-                for step in range(SECOND_BANKS):
-                    if 0 <= T < PIXEL_TILES:
-                        words_to_partitions(T, step)
-                    if T >= 1 and step >= 1:
-                        multiply(T - 1, step - 1)
+        prepare_upper_half()
+        for T in range(-1, PIXEL_TILES + 1):
+            if T + 1 < PIXEL_TILES:
+                patches_to_pixels(T + 1)
+            if T == -1:
+                prepare_lower_half()
+            for first in range(0, SECOND_BANKS, SECOND_POOL):
                 if 0 <= T < PIXEL_TILES:
-                    quantise(T)
+                    for j in range(first, min(first + SECOND_POOL, SECOND_BANKS)):
+                        words_to_partitions(T, j)
+                if T >= 1:
+                    for i in range(first, min(first + SECOND_POOL, O_TILES)):
+                        multiply(T - 1, i)
+            if 0 <= T < PIXEL_TILES:
+                quantise(T)

@@ -37,8 +37,7 @@ O_TILES = O // P
 BANK_PASSES = BANK_F32 // (P * HALVES)
 SECOND_BANKS = -(-PASSES // BANK_PASSES)
 SECOND_POOL = 2
-
-SCALAR_CHANNEL_TILES = 4
+EARLY_BANKS = 2
 
 HALF_TILES = PIXEL_TILES // 2
 STATS = 6
@@ -231,6 +230,7 @@ def tile_norm_conv_kernel(tc, a, conv_kernel_words, conv_kernel_scales, out):
         codes = keep.tile([P, PIXEL_TILES, PASSES, P], U32, align_bytes=64)
         code_scales = keep.tile([P, PIXEL_TILES, PASSES, P], U8, align_bytes=64)
         normed_tiles = {}
+        sorted_tiles = {}
         grouped_tiles = {}
         sum_tiles = {}
 
@@ -238,44 +238,42 @@ def tile_norm_conv_kernel(tc, a, conv_kernel_words, conv_kernel_scales, out):
             normed = work.tile([P, PATCH], BF16, tag="normed")
             normed_tiles[T] = normed
             by_channel = normed[:].rearrange("p (c k) -> p c k", k=TAPS)
-            banks = [first_banks.tile([P, BANK_BF16], BF16, tag="first", name="bank") for b in range(CHANNEL_TILES)]
-            for tap in range(TAPS):
-                kh, kw = divmod(tap, 3)
-                start = (TILE_ROWS * T + kh) * SIDE
-                for b in range(CHANNEL_TILES):
+            for channel_tiles in (range(0, EARLY_BANKS), range(EARLY_BANKS, CHANNEL_TILES)):
+                banks = {}
+                for b in channel_tiles:
+                    banks[b] = first_banks.tile([P, BANK_BF16], BF16, tag="first", name="bank")
+                for tap in range(TAPS):
+                    kh, kw = divmod(tap, 3)
+                    start = (TILE_ROWS * T + kh) * SIDE
+                    for b in channel_tiles:
+                        first, count, loaded_from = channel_tile(b)
+                        own_channels_first = ident_bf if first == loaded_from else ident_turned
+                        nc.tensor.transpose(
+                            out=banks[b][:, tap * BANK_CHANNELS : tap * BANK_CHANNELS + P],
+                            in_=shifted[:, kw, b, start : start + P],
+                            identity=own_channels_first[:],
+                        )
+                for b in channel_tiles:
                     first, count, loaded_from = channel_tile(b)
-                    own_channels_first = ident_bf if first == loaded_from else ident_turned
-                    nc.tensor.transpose(
-                        out=banks[b][:, tap * BANK_CHANNELS : tap * BANK_CHANNELS + P],
-                        in_=shifted[:, kw, b, start : start + P],
-                        identity=own_channels_first[:],
-                    )
-            for b in range(CHANNEL_TILES):
-                first, count, loaded_from = channel_tile(b)
-                raw = banks[b][:, 0 : TAPS * BANK_CHANNELS].rearrange("p (k c) -> p c k", k=TAPS)[:, 0:count, :]
-                if b < SCALAR_CHANNEL_TILES:
                     nc.scalar.activation(
                         out=by_channel[:, first : first + count, :],
-                        in_=raw,
+                        in_=banks[b][:, 0 : TAPS * BANK_CHANNELS].rearrange("p (k c) -> p c k", k=TAPS)[:, 0:count, :],
                         func=ACT.Identity,
                         bias=shift[:, T : T + 1],
                         scale=inv_std[:, T : T + 1],
                     )
-                else:
-                    nc.vector.tensor_scalar(
-                        out=by_channel[:, first : first + count, :],
-                        in0=raw,
-                        scalar1=inv_std[:, T : T + 1],
-                        scalar2=shift[:, T : T + 1],
-                        op0=ALU.mult,
-                        op1=ALU.add,
-                    )
+
+        def sort_words(T):
+            sorted_tiles[T] = work.tile([P, PASSES, HALVES, P], F32, tag="sorted", name="sorted_words")
+            nc.vector.tensor_copy(
+                out=sorted_tiles[T][:],
+                in_=normed_tiles[T][:].bitcast(F32).rearrange("p (g r u) -> p g u r", g=PASSES, u=HALVES),
+            )
 
         def words_to_partitions(T, j):
             if j == 0:
                 grouped_tiles[T] = work.tile([P, PASSES, P * PACK], BF16, tag="grouped", align_bytes=64, name="grouped")
             grouped_pairs = grouped_tiles[T][:].bitcast(F32).rearrange("p g (n u) -> p g n u", u=HALVES)
-            normed_pairs = normed_tiles[T][:].bitcast(F32)
             pass_pairs = P * HALVES
             g0 = j * BANK_PASSES
             n = min(BANK_PASSES, PASSES - g0)
@@ -284,7 +282,7 @@ def tile_norm_conv_kernel(tc, a, conv_kernel_words, conv_kernel_scales, out):
                 for u in range(HALVES):
                     nc.tensor.transpose(
                         out=bank[:, (i * HALVES + u) * P : (i * HALVES + u + 1) * P],
-                        in_=normed_pairs[:, (g0 + i) * pass_pairs + u : (g0 + i + 1) * pass_pairs : HALVES],
+                        in_=sorted_tiles[T][:, g0 + i, u, :],
                         identity=ident_f32[:],
                     )
             nc.vector.tensor_copy(
@@ -339,3 +337,5 @@ def tile_norm_conv_kernel(tc, a, conv_kernel_words, conv_kernel_scales, out):
                         multiply(T - 1, i)
             if 0 <= T < PIXEL_TILES:
                 quantise(T)
+            if T + 1 < PIXEL_TILES:
+                sort_words(T + 1)

@@ -37,7 +37,9 @@ O_TILES = O // P
 BANK_PASSES = BANK_F32 // (P * HALVES)
 SECOND_BANKS = -(-PASSES // BANK_PASSES)
 SECOND_POOL = 2
-EARLY_BANKS = 2
+RUN = 4
+
+SCALAR_CHANNEL_TILES = 4
 
 HALF_TILES = PIXEL_TILES // 2
 STATS = 6
@@ -230,50 +232,52 @@ def tile_norm_conv_kernel(tc, a, conv_kernel_words, conv_kernel_scales, out):
         codes = keep.tile([P, PIXEL_TILES, PASSES, P], U32, align_bytes=64)
         code_scales = keep.tile([P, PIXEL_TILES, PASSES, P], U8, align_bytes=64)
         normed_tiles = {}
-        sorted_tiles = {}
         grouped_tiles = {}
         sum_tiles = {}
 
         def patches_to_pixels(T):
             normed = work.tile([P, PATCH], BF16, tag="normed")
             normed_tiles[T] = normed
-            by_channel = normed[:].rearrange("p (c k) -> p c k", k=TAPS)
-            for channel_tiles in (range(0, EARLY_BANKS), range(EARLY_BANKS, CHANNEL_TILES)):
-                banks = {}
-                for b in channel_tiles:
-                    banks[b] = first_banks.tile([P, BANK_BF16], BF16, tag="first", name="bank")
-                for tap in range(TAPS):
-                    kh, kw = divmod(tap, 3)
-                    start = (TILE_ROWS * T + kh) * SIDE
-                    for b in channel_tiles:
-                        first, count, loaded_from = channel_tile(b)
-                        own_channels_first = ident_bf if first == loaded_from else ident_turned
-                        nc.tensor.transpose(
-                            out=banks[b][:, tap * BANK_CHANNELS : tap * BANK_CHANNELS + P],
-                            in_=shifted[:, kw, b, start : start + P],
-                            identity=own_channels_first[:],
-                        )
-                for b in channel_tiles:
+            by_run = normed[:].rearrange("p (c i k) -> p c k i", i=RUN, k=TAPS)
+            banks = [first_banks.tile([P, BANK_BF16], BF16, tag="first", name="bank") for b in range(CHANNEL_TILES)]
+            for tap in range(TAPS):
+                kh, kw = divmod(tap, 3)
+                start = (TILE_ROWS * T + kh) * SIDE
+                for b in range(CHANNEL_TILES):
                     first, count, loaded_from = channel_tile(b)
+                    own_channels_first = ident_bf if first == loaded_from else ident_turned
+                    nc.tensor.transpose(
+                        out=banks[b][:, tap * BANK_CHANNELS : tap * BANK_CHANNELS + P],
+                        in_=shifted[:, kw, b, start : start + P],
+                        identity=own_channels_first[:],
+                    )
+            for b in range(CHANNEL_TILES):
+                first, count, loaded_from = channel_tile(b)
+                runs = slice(first // RUN, (first + count) // RUN)
+                raw = banks[b][:, 0 : TAPS * BANK_CHANNELS].rearrange("p (k c i) -> p c k i", k=TAPS, i=RUN)[:, 0 : count // RUN]
+                if b < SCALAR_CHANNEL_TILES:
                     nc.scalar.activation(
-                        out=by_channel[:, first : first + count, :],
-                        in_=banks[b][:, 0 : TAPS * BANK_CHANNELS].rearrange("p (k c) -> p c k", k=TAPS)[:, 0:count, :],
+                        out=by_run[:, runs],
+                        in_=raw,
                         func=ACT.Identity,
                         bias=shift[:, T : T + 1],
                         scale=inv_std[:, T : T + 1],
                     )
-
-        def sort_words(T):
-            sorted_tiles[T] = work.tile([P, PASSES, HALVES, P], F32, tag="sorted", name="sorted_words")
-            nc.vector.tensor_copy(
-                out=sorted_tiles[T][:],
-                in_=normed_tiles[T][:].bitcast(F32).rearrange("p (g r u) -> p g u r", g=PASSES, u=HALVES),
-            )
+                else:
+                    nc.vector.tensor_scalar(
+                        out=by_run[:, runs],
+                        in0=raw,
+                        scalar1=inv_std[:, T : T + 1],
+                        scalar2=shift[:, T : T + 1],
+                        op0=ALU.mult,
+                        op1=ALU.add,
+                    )
 
         def words_to_partitions(T, j):
             if j == 0:
                 grouped_tiles[T] = work.tile([P, PASSES, P * PACK], BF16, tag="grouped", align_bytes=64, name="grouped")
             grouped_pairs = grouped_tiles[T][:].bitcast(F32).rearrange("p g (n u) -> p g n u", u=HALVES)
+            normed_pairs = normed_tiles[T][:].bitcast(F32)
             pass_pairs = P * HALVES
             g0 = j * BANK_PASSES
             n = min(BANK_PASSES, PASSES - g0)
@@ -282,7 +286,7 @@ def tile_norm_conv_kernel(tc, a, conv_kernel_words, conv_kernel_scales, out):
                 for u in range(HALVES):
                     nc.tensor.transpose(
                         out=bank[:, (i * HALVES + u) * P : (i * HALVES + u + 1) * P],
-                        in_=sorted_tiles[T][:, g0 + i, u, :],
+                        in_=normed_pairs[:, (g0 + i) * pass_pairs + u : (g0 + i + 1) * pass_pairs : HALVES],
                         identity=ident_f32[:],
                     )
             nc.vector.tensor_copy(
@@ -337,5 +341,3 @@ def tile_norm_conv_kernel(tc, a, conv_kernel_words, conv_kernel_scales, out):
                         multiply(T - 1, i)
             if 0 <= T < PIXEL_TILES:
                 quantise(T)
-            if T + 1 < PIXEL_TILES:
-                sort_words(T + 1)

import concourse.mybir as mybir
from concourse.masks import make_identity

BF16 = mybir.dt.bfloat16
F32 = mybir.dt.float32
I32 = mybir.dt.int32
U32 = mybir.dt.uint32
U8 = mybir.dt.uint8
FP8X4 = mybir.dt.float8_e4m3fn_x4
ALU = mybir.AluOpType
ACT = mybir.ActivationFunctionType
AXIS = mybir.AxisListType

P = 128
C = 512
SIDE = 32
PIXELS = SIDE * SIDE
TAPS = 9
O = 512
PATCH = C * TAPS
PACK = 4
PASSES = PATCH // (P * PACK)
PAIR = 2
HALVES = PACK // PAIR

PIXEL_TILES = PIXELS // P
TILE_ROWS = P // SIDE
PADDED_ROWS = SIDE + 2
IMAGE = PADDED_ROWS * SIDE

BANK_BF16 = 1024
BANK_F32 = 512
BANK_CHANNELS = (BANK_BF16 - P) // (TAPS - 1)
CHANNEL_TILES = -(-C // BANK_CHANNELS)

O_TILES = O // P
BANK_PASSES = BANK_F32 // (P * HALVES)
SECOND_BANKS = -(-PASSES // BANK_PASSES)
SECOND_POOL = 2
RUN = 4

SCALAR_CHANNEL_TILES = 4

HALF_TILES = PIXEL_TILES // 2
STATS = 6
PARITY_COUNT = C // 2

FLOPS = 2 * PIXELS * PATCH * O


def channel_tile(b):
    first = b * BANK_CHANNELS
    count = min(BANK_CHANNELS, C - first)
    loaded_from = min(first, C - P)
    return first, count, loaded_from


def tile_norm_conv_kernel(tc, a, conv_kernel_words, conv_kernel_scales, out):
    nc = tc.nc
    a_rows = a.rearrange("b c h w -> (b c) (h w)")
    out_rows = out.rearrange("b o h w -> (b o) (h w)")

    with (
        tc.tile_pool(name="keep", bufs=1) as keep,
        tc.tile_pool(name="work", bufs=2) as work,
        tc.psum_pool(name="first_banks", bufs=CHANNEL_TILES) as first_banks,
        tc.psum_pool(name="second_banks", bufs=SECOND_POOL) as second_banks,
        tc.psum_pool(name="sum_banks", bufs=1) as sum_banks,
        tc.manual_schedule(),
    ):
        shifted = keep.tile([P, 3, CHANNEL_TILES, IMAGE], BF16)
        grid = shifted[:].rearrange("p k b (y x) -> p k b y x", x=SIDE)

        def load_rows(first_row, end_row):
            for kw in (1, 0, 2):
                move = kw - 1
                lo = first_row * SIDE + max(move, 0)
                hi = end_row * SIDE + min(move, 0)
                for b in range(CHANNEL_TILES):
                    c0 = channel_tile(b)[2]
                    nc.sync.dma_start(
                        out=shifted[:, kw, b, SIDE + lo - move : SIDE + hi - move], in_=a_rows[c0 : c0 + P, lo:hi]
                    )

        def mend_columns(first_row, end_row):
            rows = slice(first_row + 1, end_row + 1)
            nc.gpsimd.tensor_copy(out=grid[:, 0, :, rows, 0:1], in_=grid[:, 1, :, rows, 1:2])
            nc.gpsimd.tensor_copy(out=grid[:, 2, :, rows, SIDE - 1 : SIDE], in_=grid[:, 1, :, rows, SIDE - 2 : SIDE - 1])

        split_row = (HALF_TILES + 1) * TILE_ROWS
        load_rows(0, split_row)
        load_rows(split_row, SIDE)

        w_scales = keep.tile([P, PASSES, O], U8, align_bytes=64)
        nc.vector.memset(w_scales[:].rearrange("p g o -> p (g o)").bitcast(I32), 0)
        for quadrant in range(4):
            nc.sync.dma_start(
                out=w_scales[32 * quadrant : 32 * quadrant + 4, :, :].bitcast(I32),
                in_=conv_kernel_scales[:, 4 * quadrant : 4 * quadrant + 4, :]
                .rearrange("g q o -> q g o")
                .bitcast(I32),
            )
        w_words = keep.tile([P, PASSES, O], U32, align_bytes=64)
        nc.sync.dma_start(
            out=w_words[:].bitcast(I32),
            in_=conv_kernel_words.rearrange("g r o t -> r g (o t)").bitcast(I32),
        )

        one = keep.tile([P, 1], F32)
        nc.vector.memset(one[:], 1.0)
        nc.scalar.activation(out=one[:], in_=one[:], func=ACT.Sqrt)

        ident_bf = keep.tile([P, P], BF16)
        make_identity(nc, ident_bf[:])
        ident_f32 = keep.tile([P, P], F32)
        make_identity(nc, ident_f32[:])
        turn = channel_tile(CHANNEL_TILES - 1)[0] - channel_tile(CHANNEL_TILES - 1)[2]
        ident_turned = keep.tile([P, P], BF16)
        nc.vector.tensor_copy(out=ident_turned[:, 0 : P - turn], in_=ident_bf[:, turn:P])
        nc.vector.tensor_copy(out=ident_turned[:, P - turn : P], in_=ident_bf[:, 0:turn])

        ident_rows = ident_f32[:].rearrange("p (y x) -> p y x", x=SIDE)
        ident_padded = keep.tile([P, TILE_ROWS, SIDE + 2], F32)
        nc.vector.tensor_copy(out=ident_padded[:, :, 1 : SIDE + 1], in_=ident_rows)
        nc.vector.tensor_copy(out=ident_padded[:, :, 0:1], in_=ident_rows[:, :, 1:2])
        nc.vector.tensor_copy(out=ident_padded[:, :, SIDE + 1 : SIDE + 2], in_=ident_rows[:, :, SIDE - 2 : SIDE - 1])
        band = keep.tile([P, 3 * TILE_ROWS + 2, SIDE], F32)
        nc.vector.memset(band[:], 0.0)
        across = band[:, TILE_ROWS + 1 : 2 * TILE_ROWS + 1, :]
        nc.vector.tensor_add(out=across, in0=ident_padded[:, :, 0:SIDE], in1=ident_padded[:, :, 1 : SIDE + 1])
        nc.vector.tensor_add(out=across, in0=across, in1=ident_padded[:, :, 2 : SIDE + 2])
        box = keep.tile([P, 3 * TILE_ROWS, SIDE], F32)
        nc.vector.tensor_add(out=box[:], in0=band[:, 0 : 3 * TILE_ROWS, :], in1=band[:, 1 : 3 * TILE_ROWS + 1, :])
        nc.vector.tensor_add(out=box[:], in0=box[:], in1=band[:, 2 : 3 * TILE_ROWS + 2, :])
        box_to_tile_above = box[:, 0:TILE_ROWS, :].rearrange("p y x -> p (y x)")
        box_same_tile = box[:, TILE_ROWS : 2 * TILE_ROWS, :].rearrange("p y x -> p (y x)")
        box_to_tile_below = box[:, 2 * TILE_ROWS : 3 * TILE_ROWS, :].rearrange("p y x -> p (y x)")
        reflect_top = keep.tile([P, TILE_ROWS, SIDE], F32)
        nc.vector.memset(reflect_top[:], 0.0)
        nc.vector.tensor_copy(out=reflect_top[:, 0:1, :], in_=across[:, 1:2, :])
        reflect_bottom = keep.tile([P, TILE_ROWS, SIDE], F32)
        nc.vector.memset(reflect_bottom[:], 0.0)
        nc.vector.tensor_copy(
            out=reflect_bottom[:, TILE_ROWS - 1 : TILE_ROWS, :], in_=across[:, TILE_ROWS - 2 : TILE_ROWS - 1, :]
        )

        pixel_stats = keep.tile([P, PIXEL_TILES + 2, STATS], F32)
        nc.vector.memset(pixel_stats[:], 0.0)
        by_parity = pixel_stats[:].rearrange("p T (e s) -> p T e s", e=2)
        inv_std = keep.tile([P, PIXEL_TILES], F32)
        shift = keep.tile([P, PIXEL_TILES], F32)

        def pixel_statistics(first_tile, end_tile):
            for T in range(first_tile, end_tile):
                start = (TILE_ROWS * T + 1) * SIDE
                by_pixel = second_banks.tile([P, BANK_BF16], BF16, tag="second")
                for b in range(CHANNEL_TILES):
                    c0 = channel_tile(b)[2]
                    nc.tensor.transpose(
                        out=by_pixel[:, c0 : c0 + P], in_=shifted[:, 1, b, start : start + P], identity=ident_bf[:]
                    )
                nc.vector.bn_stats(out=pixel_stats[:, 1 + T, :], in_=by_pixel[:, 0:C])
            tiles = slice(1 + first_tile, 1 + end_tile)
            squared_means = work.tile([P, end_tile - first_tile, 2], F32, tag="squared_means")
            nc.vector.tensor_mul(out=squared_means[:], in0=by_parity[:, tiles, :, 1], in1=by_parity[:, tiles, :, 1])
            nc.vector.scalar_tensor_tensor(
                out=by_parity[:, tiles, :, 2],
                in0=squared_means[:],
                scalar=float(PARITY_COUNT),
                in1=by_parity[:, tiles, :, 2],
                op0=ALU.mult,
                op1=ALU.add,
            )

        def patch_statistics(first_tile, end_tile):
            n = end_tile - first_tile
            bank = sum_banks.tile([P, BANK_F32], F32, tag="sums")
            boxed = bank[:, 0 : 4 * n].rearrange("p (T e s) -> p T e s", e=2, s=2)

            def neighbours(offset):
                return by_parity[:, 1 + first_tile + offset : 1 + end_tile + offset, :, 1:3]

            terms = [
                (boxed, box_same_tile, neighbours(0)),
                (boxed, box_to_tile_below, neighbours(-1)),
                (boxed, box_to_tile_above, neighbours(1)),
            ]
            if first_tile == 0:
                terms.append((boxed[:, 0:1], reflect_top[:].rearrange("p y x -> p (y x)"), neighbours(0)[:, 0:1]))
            if end_tile == PIXEL_TILES:
                terms.append(
                    (boxed[:, n - 1 : n], reflect_bottom[:].rearrange("p y x -> p (y x)"), neighbours(0)[:, n - 1 : n])
                )
            for i, (target, matrix, numbers) in enumerate(terms):
                nc.tensor.matmul(out=target, lhsT=matrix, rhs=numbers, start=(i == 0), stop=(i == len(terms) - 1))
            patch = work.tile([P, n, 2], F32, tag="patch")
            nc.vector.tensor_reduce(out=patch[:], in_=boxed.rearrange("p T e s -> p T s e"), axis=AXIS.X, op=ALU.add)
            deviations = work.tile([P, n], F32, tag="deviations")
            nc.vector.tensor_mul(out=deviations[:], in0=patch[:, :, 0], in1=patch[:, :, 0])
            nc.vector.scalar_tensor_tensor(
                out=deviations[:],
                in0=deviations[:],
                scalar=-float(PARITY_COUNT * PARITY_COUNT) / PATCH,
                in1=patch[:, :, 1],
                op0=ALU.mult,
                op1=ALU.add,
            )
            std = work.tile([P, n], F32, tag="std")
            nc.scalar.activation(out=std[:], in_=deviations[:], func=ACT.Sqrt, scale=1.0 / (PATCH - 1))
            nc.vector.reciprocal(out=inv_std[:, first_tile:end_tile], in_=std[:])
            nc.vector.scalar_tensor_tensor(
                out=shift[:, first_tile:end_tile],
                in0=patch[:, :, 0],
                scalar=-float(PARITY_COUNT) / PATCH,
                in1=inv_std[:, first_tile:end_tile],
                op0=ALU.mult,
                op1=ALU.mult,
            )

        def prepare_upper_half():
            mend_columns(0, split_row)
            pixel_statistics(0, HALF_TILES + 1)
            nc.vector.tensor_copy(out=grid[:, :, :, 0, :], in_=grid[:, :, :, 2, :])
            patch_statistics(0, HALF_TILES)

        def prepare_lower_half():
            mend_columns(split_row, SIDE)
            pixel_statistics(HALF_TILES + 1, PIXEL_TILES)
            nc.vector.tensor_copy(out=grid[:, :, :, SIDE + 1, :], in_=grid[:, :, :, SIDE - 1, :])
            patch_statistics(HALF_TILES, PIXEL_TILES)

        codes = keep.tile([P, PIXEL_TILES, PASSES, P], U32, align_bytes=64)
        code_scales = keep.tile([P, PIXEL_TILES, PASSES, P], U8, align_bytes=64)
        normed_tiles = {}
        grouped_tiles = {}
        sum_tiles = {}

        def patches_to_pixels(T):
            normed = work.tile([P, PATCH], BF16, tag="normed")
            normed_tiles[T] = normed
            by_run = normed[:].rearrange("p (c i k) -> p c k i", i=RUN, k=TAPS)
            banks = [first_banks.tile([P, BANK_BF16], BF16, tag="first", name="bank") for b in range(CHANNEL_TILES)]
            for tap in range(TAPS):
                kh, kw = divmod(tap, 3)
                start = (TILE_ROWS * T + kh) * SIDE
                for b in range(CHANNEL_TILES):
                    first, count, loaded_from = channel_tile(b)
                    own_channels_first = ident_bf if first == loaded_from else ident_turned
                    nc.tensor.transpose(
                        out=banks[b][:, tap * BANK_CHANNELS : tap * BANK_CHANNELS + P],
                        in_=shifted[:, kw, b, start : start + P],
                        identity=own_channels_first[:],
                    )
            for b in range(CHANNEL_TILES):
                first, count, loaded_from = channel_tile(b)
                runs = slice(first // RUN, (first + count) // RUN)
                raw = banks[b][:, 0 : TAPS * BANK_CHANNELS].rearrange("p (k c i) -> p c k i", k=TAPS, i=RUN)[:, 0 : count // RUN]
                if b < SCALAR_CHANNEL_TILES:
                    nc.scalar.activation(
                        out=by_run[:, runs],
                        in_=raw,
                        func=ACT.Identity,
                        bias=shift[:, T : T + 1],
                        scale=inv_std[:, T : T + 1],
                    )
                else:
                    nc.vector.tensor_scalar(
                        out=by_run[:, runs],
                        in0=raw,
                        scalar1=inv_std[:, T : T + 1],
                        scalar2=shift[:, T : T + 1],
                        op0=ALU.mult,
                        op1=ALU.add,
                    )

        def words_to_partitions(T, j):
            if j == 0:
                grouped_tiles[T] = work.tile([P, PASSES, P * PACK], BF16, tag="grouped", align_bytes=64, name="grouped")
            grouped_pairs = grouped_tiles[T][:].bitcast(F32).rearrange("p g (n u) -> p g n u", u=HALVES)
            normed_pairs = normed_tiles[T][:].bitcast(F32)
            pass_pairs = P * HALVES
            g0 = j * BANK_PASSES
            n = min(BANK_PASSES, PASSES - g0)
            bank = second_banks.tile([P, BANK_F32], F32, tag="second")
            for i in range(n):
                for u in range(HALVES):
                    nc.tensor.transpose(
                        out=bank[:, (i * HALVES + u) * P : (i * HALVES + u + 1) * P],
                        in_=normed_pairs[:, (g0 + i) * pass_pairs + u : (g0 + i + 1) * pass_pairs : HALVES],
                        identity=ident_f32[:],
                    )
            nc.vector.tensor_copy(
                out=grouped_pairs[:, g0 : g0 + n, :, :],
                in_=bank[:, 0 : n * pass_pairs].rearrange("p (g u n) -> p g n u", g=n, u=HALVES),
            )

        def quantise(T):
            passes_in_call = 8
            for g0 in range(0, PASSES, passes_in_call):
                n = min(passes_in_call, PASSES - g0)
                nc.vector.quantize_mx(
                    out=codes[:, T, g0 : g0 + n, :].rearrange("p g n -> p (g n)").bitcast(FP8X4),
                    scales=code_scales[:, T, g0 : g0 + n, :].rearrange("p g n -> p (g n)"),
                    in_=grouped_tiles[T][:, g0 : g0 + n, :].rearrange("p g n -> p (g n)"),
                )

        def multiply(T, i):
            if i == 0:
                sum_tiles[T] = sum_banks.tile([P, O_TILES, P], F32, tag="sums", name="sums")
            sums = sum_tiles[T]
            o_columns = slice(i * P, (i + 1) * P)
            for g in range(PASSES):
                nc.tensor.matmul_mx(
                    out=sums[:, i, :],
                    lhsT=w_words[:, g, o_columns].bitcast(FP8X4),
                    lhsT_scale=w_scales[:, g, o_columns],
                    rhs=codes[:, T, g, :].bitcast(FP8X4),
                    rhs_scale=code_scales[:, T, g, :],
                    start=(g == 0),
                    stop=(g == PASSES - 1),
                )
            if i == O_TILES - 1:
                result = work.tile([P, O_TILES, P], F32)
                nc.scalar.copy(out=result[:], in_=sums[:])
                nc.sync.dma_start(
                    out=out_rows[:, T * P : (T + 1) * P].rearrange("(i o) n -> o i n", o=P), in_=result[:]
                )

        prepare_upper_half()
        for T in range(-1, PIXEL_TILES + 1):
            if T + 1 < PIXEL_TILES:
                patches_to_pixels(T + 1)
            if T == -1:
                prepare_lower_half()
            for first in range(0, SECOND_BANKS, SECOND_POOL):
                if 0 <= T < PIXEL_TILES:
                    for j in range(first, min(first + SECOND_POOL, SECOND_BANKS)):
                        words_to_partitions(T, j)
                if T >= 1:
                    for i in range(first, min(first + SECOND_POOL, O_TILES)):
                        multiply(T - 1, i)
            if 0 <= T < PIXEL_TILES:
                quantise(T)
